import numpy as np
import ml_dtypes


def mxq(x, axis, fmt="e4m3"):
    dtype, down = {"e4m3": (ml_dtypes.float8_e4m3fn, 7), "e5m2": (ml_dtypes.float8_e5m2, 14)}[fmt]
    v = np.moveaxis(np.asarray(x, np.float32).astype(ml_dtypes.bfloat16).astype(np.float64), axis, -1)
    blocks = v.reshape(v.shape[:-1] + (-1, 32))
    amax = np.abs(blocks).max(-1, keepdims=True)
    byte = np.maximum(np.where(amax > 0, np.frexp(amax)[1] - 1 + 127, 0) - down, 1)
    scale = np.exp2(byte - 127.0)
    codes = (blocks / scale).astype(np.float32).astype(dtype).astype(np.float64)
    return np.moveaxis((codes * scale).reshape(v.shape), -1, axis)


WIDE = False


def mx_kscale(k):
    if not WIDE:
        return np.ones(k)
    levels = np.array([10, -10, 5, -5, 0])
    a = np.random.permutation(np.resize(levels, k // 512 * 4)).reshape(k // 512, 4)
    idx = np.arange(k)
    return np.exp2(a[idx // 512, idx % 128 // 32])


BF16 = ml_dtypes.bfloat16


def bf(x):
    return np.asarray(x, np.float32).astype(BF16)


def f64(x):
    return np.asarray(x).astype(np.float64)


B, S, D = 1, 512, 2048
ROPE_BASE = 10000.0


def rope_tables():
    inv_freq = 1.0 / ROPE_BASE ** (np.arange(0, D, 2) / D)
    freqs = np.outer(np.arange(S), inv_freq)
    emb = np.concatenate([freqs, freqs], axis=-1)
    return np.cos(emb), np.sin(emb)


def rotate_half(u):
    u1, u2 = np.split(u, 2, axis=-1)
    return np.concatenate([-u2, u1], axis=-1)


def setup_inputs():
    s = mx_kscale(D)
    c, sn = rope_tables()
    w = 1.0 / np.sqrt(D)
    return {"x": bf(np.random.standard_normal((B, S, D)) * s),
            "cos": bf(c),
            "sin": bf(sn),
            "Wq": bf(np.random.standard_normal((D, D)) * w / s[None, :]),
            "Wk": bf(np.random.standard_normal((D, D)) * w / s[None, :])}


def reference(x, cos, sin, Wq, Wk):
    xq = mxq(f64(x), 2, "e4m3")
    q = xq @ mxq(f64(Wq), 1, "e4m3").T
    k = xq @ mxq(f64(Wk), 1, "e4m3").T
    c, sn = f64(cos), f64(sin)
    q_rot = q * c + rotate_half(q) * sn
    k_rot = k * c + rotate_half(k) * sn
    return q_rot, k_rot

@@ -1,0 +1,168 @@
+from contextlib import ExitStack
+
+import concourse.mybir as mybir
+from concourse.masks import make_identity
+
+BF16 = mybir.dt.bfloat16
+F32 = mybir.dt.float32
+U32 = mybir.dt.uint32
+U8 = mybir.dt.uint8
+FP8X4 = mybir.dt.float8_e4m3fn_x4
+ALU = mybir.AluOpType
+
+P = 128
+TOKENS = 512
+D = 2048
+FLOPS = 2 * 2 * TOKENS * D * D
+
+TOKEN_TILES = TOKENS // P
+K_PASS = 4 * P
+PASSES = D // K_PASS
+WORDS = K_PASS // 2
+PART = 512
+BLOCK = 256
+HALVES = 2
+COLUMN_HALVES = D // (HALVES * PART)
+STEPS_PER_GROUP = 4
+RAW_BUFS = 8
+
+
+def tile_attention_pa_kernel(tc, x, cos, sin, Wq, Wk, out_0, out_1):
+    nc = tc.nc
+
+    x_blocks = x[0].rearrange("(p b r) k -> b p r k", b=2, r=2)
+    w_blocks = [w.rearrange("(b p r) k -> b p r k", p=P, r=2) for w in (Wq, Wk)]
+    table_view = "(p a) (h c w) -> c p a h w"
+    cos_cols = cos.rearrange(table_view, a=TOKEN_TILES, h=HALVES, c=COLUMN_HALVES)
+    sin_cols = sin.rearrange(table_view, a=TOKEN_TILES, h=HALVES, c=COLUMN_HALVES)
+    out_view = "(p a) (h c w) -> c a p h w"
+    out_cols = [
+        o[0].rearrange(out_view, a=TOKEN_TILES, h=HALVES, c=COLUMN_HALVES) for o in (out_0, out_1)
+    ]
+
+    parts = [(m, c, h) for c in range(COLUMN_HALVES) for m in range(2) for h in range(HALVES)]
+    w_block_list = [(m, 4 * h + 2 * c + r2) for (m, c, h) in parts for r2 in range(2)]
+    raw_sources = [x_blocks[0], x_blocks[1]] + [w_blocks[m][b] for (m, b) in w_block_list]
+
+    with ExitStack() as ctx:
+        const = ctx.enter_context(tc.tile_pool(name="const", bufs=1))
+        raw_pool = ctx.enter_context(tc.tile_pool(name="raw", bufs=RAW_BUFS))
+        grouped_pool = ctx.enter_context(tc.tile_pool(name="grouped", bufs=6))
+        w_mx_pool = ctx.enter_context(tc.tile_pool(name="w_mx", bufs=3))
+        direct_pool = ctx.enter_context(tc.tile_pool(name="direct", bufs=8))
+        crossed_pool = ctx.enter_context(tc.tile_pool(name="crossed", bufs=6))
+        flipped_pool = ctx.enter_context(tc.psum_pool(name="flipped", bufs=4))
+        acc_pool = ctx.enter_context(tc.psum_pool(name="acc", bufs=4))
+        ctx.enter_context(tc.manual_schedule())
+
+        ident = const.tile([P, P], F32)
+        make_identity(nc, ident[:])
+        x_codes = const.tile([P, PASSES, TOKENS], U32, align_bytes=64)
+        x_scales = const.tile([P, PASSES, TOKENS], U8, align_bytes=64)
+        cos_sb = [
+            const.tile([P, TOKEN_TILES, HALVES, PART], BF16, name="cos_sb%d" % c)
+            for c in range(COLUMN_HALVES)
+        ]
+        sin_sb = [
+            const.tile([P, TOKEN_TILES, HALVES, PART], BF16, name="sin_sb%d" % c)
+            for c in range(COLUMN_HALVES)
+        ]
+
+        raw_tiles = {}
+
+        def load_raw(j):
+            if j < len(raw_sources):
+                raw = raw_pool.tile([P, 2, D], BF16, name="raw")
+                nc.sync.dma_start(out=raw[:], in_=raw_sources[j])
+                raw_tiles[j] = raw
+
+        def load_tables(c):
+            nc.sync.dma_start(out=cos_sb[c][:], in_=cos_cols[c])
+            nc.sync.dma_start(out=sin_sb[c][:], in_=sin_cols[c])
+
+        def quantise_block(j, column_order, codes, scales):
+            words = raw_tiles[j][:].bitcast(F32)
+            for g in range(PASSES):
+                flipped = flipped_pool.tile([P, 2, 2, P], F32)
+                for u in range(2):
+                    for r in range(2):
+                        lo = WORDS * g + P * u
+                        nc.tensor.transpose(flipped[:, u, r, :], words[:, r, lo : lo + P], ident[:])
+                grouped = grouped_pool.tile([P, 4 * BLOCK], BF16, align_bytes=64)
+                in_order = "kp (%s u) -> kp %s u" % (column_order, column_order)
+                nc.scalar.copy(
+                    out=grouped[:].bitcast(F32).rearrange(in_order, r=2, u=2),
+                    in_=flipped[:].rearrange("kp u r f -> kp %s u" % column_order),
+                )
+                nc.vector.quantize_mx(
+                    out=codes[:, g, :].bitcast(FP8X4), scales=scales[:, g, :], in_=grouped[:]
+                )
+            load_raw(j + RAW_BUFS)
+
+        def quantise_w_block(i):
+            if i >= len(w_block_list):
+                return
+            if i % 2 == 0:
+                w_codes = w_mx_pool.tile([P, PASSES, PART], U32, align_bytes=64, name="w_codes")
+                w_scales = w_mx_pool.tile([P, PASSES, PART], U8, align_bytes=64, name="w_scales")
+                w_mx[i // 2] = (w_codes, w_scales)
+            w_codes, w_scales = w_mx[i // 2]
+            cols = slice(BLOCK * (i % 2), BLOCK * (i % 2) + BLOCK)
+            quantise_block(2 + i, "f r", w_codes[:, :, cols], w_scales[:, :, cols])
+
+        w_mx = {}
+        direct = {}
+        crossed = {}
+
+        for j in range(6):
+            load_raw(j)
+        load_tables(0)
+        for j in range(6, RAW_BUFS):
+            load_raw(j)
+
+        for b in range(2):
+            cols = slice(BLOCK * b, BLOCK * b + BLOCK)
+            quantise_block(b, "r f", x_codes[:, :, cols], x_scales[:, :, cols])
+
+        quantise_w_block(0)
+        quantise_w_block(1)
+
+        last_step = 2 * len(parts) - 1
+        for step in range(last_step + 1):
+            part = step // 2
+            m, c, h = parts[part]
+            if step == STEPS_PER_GROUP:
+                load_tables(1)
+            quantise_w_block(step + 2)
+            w_codes, w_scales = w_mx[part]
+            for a in (2 * (step % 2), 2 * (step % 2) + 1):
+                acc = acc_pool.tile([P, PART], F32)
+                tok = slice(P * a, P * a + P)
+                for g in range(PASSES):
+                    nc.tensor.matmul_mx(
+                        out=acc[:],
+                        lhsT=x_codes[:, g, tok].bitcast(FP8X4),
+                        lhsT_scale=x_scales[:, g, tok],
+                        rhs=w_codes[:, g, :].bitcast(FP8X4),
+                        rhs_scale=w_scales[:, g, :],
+                        start=(g == 0),
+                        stop=(g == PASSES - 1),
+                    )
+                if h == 0:
+                    direct[a] = direct_pool.tile([P, HALVES, PART], F32, name="direct")
+                    crossed[a] = crossed_pool.tile([P, HALVES, PART], F32, name="crossed")
+                nc.vector.tensor_tensor(
+                    out=direct[a][:, h, :], in0=acc[:], in1=cos_sb[c][:, a, h, :], op=ALU.mult
+                )
+                nc.vector.tensor_tensor(
+                    out=crossed[a][:, 1 - h, :], in0=acc[:], in1=sin_sb[c][:, a, 1 - h, :], op=ALU.mult
+                )
+                if h == 1:
+                    adder = nc.vector if step == last_step else nc.gpsimd
+                    adder.tensor_tensor(
+                        out=direct[a][:, 0, :], in0=direct[a][:, 0, :], in1=crossed[a][:, 0, :], op=ALU.subtract
+                    )
+                    adder.tensor_tensor(
+                        out=direct[a][:, 1, :], in0=direct[a][:, 1, :], in1=crossed[a][:, 1, :], op=ALU.add
+                    )
+                    nc.sync.dma_start(out=out_cols[m][c][a], in_=direct[a][:])

@@ -20,18 +20,17 @@ K_PASS = 4 * P
 PASSES = D // K_PASS
 WORDS = K_PASS // 2
 PART = 512
-BLOCK = 256
+SLAB = 256
 HALVES = 2
 COLUMN_HALVES = D // (HALVES * PART)
-STEPS_PER_GROUP = 4
 RAW_BUFS = 8
 
 
 def tile_attention_pa_kernel(tc, x, cos, sin, Wq, Wk, out_0, out_1):
     nc = tc.nc
 
-    x_blocks = x[0].rearrange("(p b r) k -> b p r k", b=2, r=2)
-    w_blocks = [w.rearrange("(b p r) k -> b p r k", p=P, r=2) for w in (Wq, Wk)]
+    x_slabs = x[0].rearrange("(p b r) k -> b p r k", b=2, r=2)
+    w_slabs = [w.rearrange("(b p r) k -> b p r k", p=P, r=2) for w in (Wq, Wk)]
     table_view = "(p a) (h c w) -> c p a h w"
     cos_cols = cos.rearrange(table_view, a=TOKEN_TILES, h=HALVES, c=COLUMN_HALVES)
     sin_cols = sin.rearrange(table_view, a=TOKEN_TILES, h=HALVES, c=COLUMN_HALVES)
@@ -41,30 +40,24 @@ def tile_attention_pa_kernel(tc, x, cos, sin, Wq, Wk, out_0, out_1):
     ]
 
     parts = [(m, c, h) for c in range(COLUMN_HALVES) for m in range(2) for h in range(HALVES)]
-    w_block_list = [(m, 4 * h + 2 * c + r2) for (m, c, h) in parts for r2 in range(2)]
-    raw_sources = [x_blocks[0], x_blocks[1]] + [w_blocks[m][b] for (m, b) in w_block_list]
+    w_slab_list = [(m, 4 * h + 2 * c + s) for (m, c, h) in parts for s in range(2)]
+    raw_sources = [x_slabs[0], x_slabs[1]] + [w_slabs[m][b] for (m, b) in w_slab_list]
 
     with ExitStack() as ctx:
         const = ctx.enter_context(tc.tile_pool(name="const", bufs=1))
         raw_pool = ctx.enter_context(tc.tile_pool(name="raw", bufs=RAW_BUFS))
-        grouped_pool = ctx.enter_context(tc.tile_pool(name="grouped", bufs=6))
-        w_mx_pool = ctx.enter_context(tc.tile_pool(name="w_mx", bufs=3))
-        direct_pool = ctx.enter_context(tc.tile_pool(name="direct", bufs=8))
-        crossed_pool = ctx.enter_context(tc.tile_pool(name="crossed", bufs=6))
+        grouped_pool = ctx.enter_context(tc.tile_pool(name="grouped", bufs=3))
+        x_mx_pool = ctx.enter_context(tc.tile_pool(name="x_mx", bufs=2))
+        w_mx_pool = ctx.enter_context(tc.tile_pool(name="w_mx", bufs=5))
+        products_pool = ctx.enter_context(tc.tile_pool(name="products", bufs=2 * TOKEN_TILES))
         flipped_pool = ctx.enter_context(tc.psum_pool(name="flipped", bufs=4))
         acc_pool = ctx.enter_context(tc.psum_pool(name="acc", bufs=4))
         ctx.enter_context(tc.manual_schedule())
 
         ident = const.tile([P, P], F32)
         make_identity(nc, ident[:])
-        x_codes = const.tile([P, PASSES, TOKENS], U32, align_bytes=64)
-        x_scales = const.tile([P, PASSES, TOKENS], U8, align_bytes=64)
-        cos_sb = [
-            const.tile([P, TOKEN_TILES, HALVES, PART], BF16, name="cos_sb%d" % c)
-            for c in range(COLUMN_HALVES)
-        ]
-        sin_sb = [
-            const.tile([P, TOKEN_TILES, HALVES, PART], BF16, name="sin_sb%d" % c)
+        tables = [
+            const.tile([P, TOKEN_TILES, 2 * HALVES, PART], BF16, name="tables%d" % c)
             for c in range(COLUMN_HALVES)
         ]
 
@@ -76,93 +69,94 @@ def tile_attention_pa_kernel(tc, x, cos, sin, Wq, Wk, out_0, out_1):
                 nc.sync.dma_start(out=raw[:], in_=raw_sources[j])
                 raw_tiles[j] = raw
 
-        def load_tables(c):
-            nc.sync.dma_start(out=cos_sb[c][:], in_=cos_cols[c])
-            nc.sync.dma_start(out=sin_sb[c][:], in_=sin_cols[c])
+        def load_tables(c, h):
+            nc.sync.dma_start(out=tables[c][:, :, 2 * h, :], in_=cos_cols[c][:, :, h, :])
+            nc.sync.dma_start(out=tables[c][:, :, 2 * h + 1, :], in_=sin_cols[c][:, :, 1 - h, :])
 
-        def quantise_block(j, column_order, codes, scales):
+        def quantise_slab(j, column_order, pool):
             words = raw_tiles[j][:].bitcast(F32)
+            grouped = grouped_pool.tile([P, PASSES, 4 * SLAB], BF16, align_bytes=64)
+            in_order = "kp (%s u) -> kp %s u" % (column_order, column_order)
             for g in range(PASSES):
                 flipped = flipped_pool.tile([P, 2, 2, P], F32)
                 for u in range(2):
                     for r in range(2):
                         lo = WORDS * g + P * u
                         nc.tensor.transpose(flipped[:, u, r, :], words[:, r, lo : lo + P], ident[:])
-                grouped = grouped_pool.tile([P, 4 * BLOCK], BF16, align_bytes=64)
-                in_order = "kp (%s u) -> kp %s u" % (column_order, column_order)
                 nc.scalar.copy(
-                    out=grouped[:].bitcast(F32).rearrange(in_order, r=2, u=2),
+                    out=grouped[:, g, :].bitcast(F32).rearrange(in_order, r=2, u=2),
                     in_=flipped[:].rearrange("kp u r f -> kp %s u" % column_order),
                 )
-                nc.vector.quantize_mx(
-                    out=codes[:, g, :].bitcast(FP8X4), scales=scales[:, g, :], in_=grouped[:]
-                )
+            codes = pool.tile([P, PASSES, SLAB], U32, align_bytes=64, name="codes")
+            scales = pool.tile([P, PASSES, SLAB], U8, align_bytes=64, name="scales")
+            nc.vector.quantize_mx(
+                out=codes[:].rearrange("kp g f -> kp (g f)").bitcast(FP8X4),
+                scales=scales[:].rearrange("kp g f -> kp (g f)"),
+                in_=grouped[:].rearrange("kp g f -> kp (g f)"),
+            )
             load_raw(j + RAW_BUFS)
-
-        def quantise_w_block(i):
-            if i >= len(w_block_list):
-                return
-            if i % 2 == 0:
-                w_codes = w_mx_pool.tile([P, PASSES, PART], U32, align_bytes=64, name="w_codes")
-                w_scales = w_mx_pool.tile([P, PASSES, PART], U8, align_bytes=64, name="w_scales")
-                w_mx[i // 2] = (w_codes, w_scales)
-            w_codes, w_scales = w_mx[i // 2]
-            cols = slice(BLOCK * (i % 2), BLOCK * (i % 2) + BLOCK)
-            quantise_block(2 + i, "f r", w_codes[:, :, cols], w_scales[:, :, cols])
+            return codes, scales
 
         w_mx = {}
-        direct = {}
-        crossed = {}
+
+        def quantise_w_slab(i):
+            if i < len(w_slab_list):
+                w_mx[i] = quantise_slab(2 + i, "f r", w_mx_pool)
 
         for j in range(6):
             load_raw(j)
-        load_tables(0)
+        load_tables(0, 0)
         for j in range(6, RAW_BUFS):
             load_raw(j)
+        load_tables(0, 1)
 
-        for b in range(2):
-            cols = slice(BLOCK * b, BLOCK * b + BLOCK)
-            quantise_block(b, "r f", x_codes[:, :, cols], x_scales[:, :, cols])
+        x_mx = [quantise_slab(b, "r f", x_mx_pool) for b in range(2)]
 
-        quantise_w_block(0)
-        quantise_w_block(1)
+        quantise_w_slab(0)
+        quantise_w_slab(1)
+        load_tables(1, 0)
+        load_tables(1, 1)
+
+        products = {}
 
         last_step = 2 * len(parts) - 1
         for step in range(last_step + 1):
             part = step // 2
             m, c, h = parts[part]
-            if step == STEPS_PER_GROUP:
-                load_tables(1)
-            quantise_w_block(step + 2)
-            w_codes, w_scales = w_mx[part]
-            for a in (2 * (step % 2), 2 * (step % 2) + 1):
+            quantise_w_slab(step + 2)
+            b = step % 2
+            x_codes, x_scales = x_mx[b]
+            for r in range(2):
+                a = 2 * b + r
+                tok = slice(P * r, P * r + P)
                 acc = acc_pool.tile([P, PART], F32)
-                tok = slice(P * a, P * a + P)
-                for g in range(PASSES):
-                    nc.tensor.matmul_mx(
-                        out=acc[:],
-                        lhsT=x_codes[:, g, tok].bitcast(FP8X4),
-                        lhsT_scale=x_scales[:, g, tok],
-                        rhs=w_codes[:, g, :].bitcast(FP8X4),
-                        rhs_scale=w_scales[:, g, :],
-                        start=(g == 0),
-                        stop=(g == PASSES - 1),
-                    )
+                for s in range(2):
+                    w_codes, w_scales = w_mx[2 * part + s]
+                    for g in range(PASSES):
+                        nc.tensor.matmul_mx(
+                            out=acc[:, SLAB * s : SLAB * s + SLAB],
+                            lhsT=x_codes[:, g, tok].bitcast(FP8X4),
+                            lhsT_scale=x_scales[:, g, tok],
+                            rhs=w_codes[:, g, :].bitcast(FP8X4),
+                            rhs_scale=w_scales[:, g, :],
+                            start=(g == 0),
+                            stop=(g == PASSES - 1),
+                        )
                 if h == 0:
-                    direct[a] = direct_pool.tile([P, HALVES, PART], F32, name="direct")
-                    crossed[a] = crossed_pool.tile([P, HALVES, PART], F32, name="crossed")
+                    products[a] = products_pool.tile([P, 2 * HALVES, PART], F32, name="products")
                 nc.vector.tensor_tensor(
-                    out=direct[a][:, h, :], in0=acc[:], in1=cos_sb[c][:, a, h, :], op=ALU.mult
-                )
-                nc.vector.tensor_tensor(
-                    out=crossed[a][:, 1 - h, :], in0=acc[:], in1=sin_sb[c][:, a, 1 - h, :], op=ALU.mult
+                    out=products[a][:, 2 * h : 2 * h + 2, :],
+                    in0=acc[:].unsqueeze(1).to_broadcast([P, 2, PART]),
+                    in1=tables[c][:, a, 2 * h : 2 * h + 2, :],
+                    op=ALU.mult,
                 )
                 if h == 1:
                     adder = nc.vector if step == last_step else nc.gpsimd
+                    q_cos = products[a][:].rearrange("p (h s) w -> p s h w", s=2)[:, 0]
                     adder.tensor_tensor(
-                        out=direct[a][:, 0, :], in0=direct[a][:, 0, :], in1=crossed[a][:, 0, :], op=ALU.subtract
+                        out=q_cos[:, 0, :], in0=q_cos[:, 0, :], in1=products[a][:, 3, :], op=ALU.subtract
                     )
                     adder.tensor_tensor(
-                        out=direct[a][:, 1, :], in0=direct[a][:, 1, :], in1=crossed[a][:, 1, :], op=ALU.add
+                        out=q_cos[:, 1, :], in0=q_cos[:, 1, :], in1=products[a][:, 1, :], op=ALU.add
                     )
-                    nc.sync.dma_start(out=out_cols[m][c][a], in_=direct[a][:])
+                    nc.sync.dma_start(out=out_cols[m][c][a], in_=q_cos)

@@ -19,10 +19,10 @@ TOKEN_TILES = TOKENS // P
 K_PASS = 4 * P
 PASSES = D // K_PASS
 WORDS = K_PASS // 2
-PART = 512
 SLAB = 256
 HALVES = 2
-COLUMN_HALVES = D // (HALVES * PART)
+TABLE_COLS = 512
+TABLE_TILES = D // (HALVES * TABLE_COLS)
 RAW_BUFS = 8
 
 
@@ -30,18 +30,18 @@ def tile_attention_pa_kernel(tc, x, cos, sin, Wq, Wk, out_0, out_1):
     nc = tc.nc
 
     x_slabs = x[0].rearrange("(p b r) k -> b p r k", b=2, r=2)
-    w_slabs = [w.rearrange("(b p r) k -> b p r k", p=P, r=2) for w in (Wq, Wk)]
-    table_view = "(p a) (h c w) -> c p a h w"
-    cos_cols = cos.rearrange(table_view, a=TOKEN_TILES, h=HALVES, c=COLUMN_HALVES)
-    sin_cols = sin.rearrange(table_view, a=TOKEN_TILES, h=HALVES, c=COLUMN_HALVES)
-    out_view = "(p a) (h c w) -> c a p h w"
+    w_slabs = [w.rearrange("(n p r) k -> n p r k", p=P, r=2) for w in (Wq, Wk)]
+    table_view = "(p b r) (h c w) -> c b p r h w"
+    cos_cols = cos.rearrange(table_view, b=2, r=2, h=HALVES, c=TABLE_TILES)
+    sin_cols = sin.rearrange(table_view, b=2, r=2, h=HALVES, c=TABLE_TILES)
+    out_view = "(p b r) (h c s w) -> c s b h p r w"
     out_cols = [
-        o[0].rearrange(out_view, a=TOKEN_TILES, h=HALVES, c=COLUMN_HALVES) for o in (out_0, out_1)
+        o[0].rearrange(out_view, b=2, r=2, h=HALVES, c=TABLE_TILES, w=SLAB) for o in (out_0, out_1)
     ]
 
-    parts = [(m, c, h) for c in range(COLUMN_HALVES) for m in range(2) for h in range(HALVES)]
-    w_slab_list = [(m, 4 * h + 2 * c + s) for (m, c, h) in parts for s in range(2)]
-    raw_sources = [x_slabs[0], x_slabs[1]] + [w_slabs[m][b] for (m, b) in w_slab_list]
+    units = [(m, c, s) for c in range(TABLE_TILES) for m in range(2) for s in range(2)]
+    w_slab_list = [(m, 4 * h + 2 * c + s) for (m, c, s) in units for h in range(HALVES)]
+    raw_sources = [x_slabs[0], x_slabs[1]] + [w_slabs[m][n] for (m, n) in w_slab_list]
 
     with ExitStack() as ctx:
         const = ctx.enter_context(tc.tile_pool(name="const", bufs=1))
@@ -49,7 +49,7 @@ def tile_attention_pa_kernel(tc, x, cos, sin, Wq, Wk, out_0, out_1):
         grouped_pool = ctx.enter_context(tc.tile_pool(name="grouped", bufs=3))
         x_mx_pool = ctx.enter_context(tc.tile_pool(name="x_mx", bufs=2))
         w_mx_pool = ctx.enter_context(tc.tile_pool(name="w_mx", bufs=5))
-        products_pool = ctx.enter_context(tc.tile_pool(name="products", bufs=2 * TOKEN_TILES))
+        products_pool = ctx.enter_context(tc.tile_pool(name="products", bufs=6))
         flipped_pool = ctx.enter_context(tc.psum_pool(name="flipped", bufs=4))
         acc_pool = ctx.enter_context(tc.psum_pool(name="acc", bufs=4))
         ctx.enter_context(tc.manual_schedule())
@@ -57,8 +57,8 @@ def tile_attention_pa_kernel(tc, x, cos, sin, Wq, Wk, out_0, out_1):
         ident = const.tile([P, P], F32)
         make_identity(nc, ident[:])
         tables = [
-            const.tile([P, TOKEN_TILES, 2 * HALVES, PART], BF16, name="tables%d" % c)
-            for c in range(COLUMN_HALVES)
+            const.tile([P, TOKEN_TILES, HALVES, 2, TABLE_COLS], BF16, name="tables%d" % c)
+            for c in range(TABLE_TILES)
         ]
 
         raw_tiles = {}
@@ -69,9 +69,11 @@ def tile_attention_pa_kernel(tc, x, cos, sin, Wq, Wk, out_0, out_1):
                 nc.sync.dma_start(out=raw[:], in_=raw_sources[j])
                 raw_tiles[j] = raw
 
-        def load_tables(c, h):
-            nc.sync.dma_start(out=tables[c][:, :, 2 * h, :], in_=cos_cols[c][:, :, h, :])
-            nc.sync.dma_start(out=tables[c][:, :, 2 * h + 1, :], in_=sin_cols[c][:, :, 1 - h, :])
+        def load_tables(c, b):
+            pair = slice(2 * b, 2 * b + 2)
+            nc.sync.dma_start(out=tables[c][:, pair, :, 0, :], in_=cos_cols[c][b])
+            for h in range(HALVES):
+                nc.sync.dma_start(out=tables[c][:, pair, h, 1, :], in_=sin_cols[c][b][:, :, 1 - h, :])
 
         def quantise_slab(j, column_order, pool):
             words = raw_tiles[j][:].bitcast(F32)
@@ -105,36 +107,34 @@ def tile_attention_pa_kernel(tc, x, cos, sin, Wq, Wk, out_0, out_1):
 
         for j in range(6):
             load_raw(j)
-        load_tables(0, 0)
-        for j in range(6, RAW_BUFS):
-            load_raw(j)
-        load_tables(0, 1)
+        for b in range(2):
+            load_tables(0, b)
+            load_raw(6 + b)
 
         x_mx = [quantise_slab(b, "r f", x_mx_pool) for b in range(2)]
 
         quantise_w_slab(0)
         quantise_w_slab(1)
-        load_tables(1, 0)
-        load_tables(1, 1)
+        for b in range(2):
+            load_tables(1, b)
 
-        products = {}
-
-        last_step = 2 * len(parts) - 1
+        last_step = 2 * len(units) - 1
         for step in range(last_step + 1):
-            part = step // 2
-            m, c, h = parts[part]
+            unit = step // 2
+            m, c, s = units[unit]
             quantise_w_slab(step + 2)
             b = step % 2
             x_codes, x_scales = x_mx[b]
+            table_cols = slice(SLAB * s, SLAB * s + SLAB)
+            products = products_pool.tile([P, 2, HALVES, 2, SLAB], F32)
             for r in range(2):
-                a = 2 * b + r
                 tok = slice(P * r, P * r + P)
-                acc = acc_pool.tile([P, PART], F32)
-                for s in range(2):
-                    w_codes, w_scales = w_mx[2 * part + s]
+                acc = acc_pool.tile([P, HALVES, SLAB], F32)
+                for h in range(HALVES):
+                    w_codes, w_scales = w_mx[2 * unit + h]
                     for g in range(PASSES):
                         nc.tensor.matmul_mx(
-                            out=acc[:, SLAB * s : SLAB * s + SLAB],
+                            out=acc[:, h, :],
                             lhsT=x_codes[:, g, tok].bitcast(FP8X4),
                             lhsT_scale=x_scales[:, g, tok],
                             rhs=w_codes[:, g, :].bitcast(FP8X4),
@@ -142,21 +142,19 @@ def tile_attention_pa_kernel(tc, x, cos, sin, Wq, Wk, out_0, out_1):
                             start=(g == 0),
                             stop=(g == PASSES - 1),
                         )
-                if h == 0:
-                    products[a] = products_pool.tile([P, 2 * HALVES, PART], F32, name="products")
                 nc.vector.tensor_tensor(
-                    out=products[a][:, 2 * h : 2 * h + 2, :],
-                    in0=acc[:].unsqueeze(1).to_broadcast([P, 2, PART]),
-                    in1=tables[c][:, a, 2 * h : 2 * h + 2, :],
+                    out=products[:, r],
+                    in0=acc[:].unsqueeze(2).to_broadcast([P, HALVES, 2, SLAB]),
+                    in1=tables[c][:, 2 * b + r, :, :, table_cols],
                     op=ALU.mult,
                 )
-                if h == 1:
-                    adder = nc.vector if step == last_step else nc.gpsimd
-                    q_cos = products[a][:].rearrange("p (h s) w -> p s h w", s=2)[:, 0]
-                    adder.tensor_tensor(
-                        out=q_cos[:, 0, :], in0=q_cos[:, 0, :], in1=products[a][:, 3, :], op=ALU.subtract
-                    )
-                    adder.tensor_tensor(
-                        out=q_cos[:, 1, :], in0=q_cos[:, 1, :], in1=products[a][:, 1, :], op=ALU.add
-                    )
-                    nc.sync.dma_start(out=out_cols[m][c][a], in_=q_cos)
+            adder = nc.vector if step == last_step else nc.gpsimd
+            for h in range(HALVES):
+                result = products[:, :, h, 0, :]
+                adder.tensor_tensor(
+                    out=result,
+                    in0=result,
+                    in1=products[:, :, 1 - h, 1, :],
+                    op=(ALU.subtract if h == 0 else ALU.add),
+                )
+                nc.sync.dma_start(out=out_cols[m][c][s][b][h], in_=result)

@@ -23,6 +23,7 @@ SLAB = 256
 HALVES = 2
 TABLE_COLS = 512
 TABLE_TILES = D // (HALVES * TABLE_COLS)
+AHEAD = 3
 RAW_BUFS = 8
 
 
@@ -48,7 +49,7 @@ def tile_attention_pa_kernel(tc, x, cos, sin, Wq, Wk, out_0, out_1):
         raw_pool = ctx.enter_context(tc.tile_pool(name="raw", bufs=RAW_BUFS))
         grouped_pool = ctx.enter_context(tc.tile_pool(name="grouped", bufs=3))
         x_mx_pool = ctx.enter_context(tc.tile_pool(name="x_mx", bufs=2))
-        w_mx_pool = ctx.enter_context(tc.tile_pool(name="w_mx", bufs=5))
+        w_mx_pool = ctx.enter_context(tc.tile_pool(name="w_mx", bufs=6))
         products_pool = ctx.enter_context(tc.tile_pool(name="products", bufs=6))
         flipped_pool = ctx.enter_context(tc.psum_pool(name="flipped", bufs=4))
         acc_pool = ctx.enter_context(tc.psum_pool(name="acc", bufs=4))
@@ -75,7 +76,7 @@ def tile_attention_pa_kernel(tc, x, cos, sin, Wq, Wk, out_0, out_1):
             for h in range(HALVES):
                 nc.sync.dma_start(out=tables[c][:, pair, h, 1, :], in_=sin_cols[c][b][:, :, 1 - h, :])
 
-        def quantise_slab(j, column_order, pool):
+        def transpose_slab(j, column_order):
             words = raw_tiles[j][:].bitcast(F32)
             grouped = grouped_pool.tile([P, PASSES, 4 * SLAB], BF16, align_bytes=64)
             in_order = "kp (%s u) -> kp %s u" % (column_order, column_order)
@@ -89,6 +90,10 @@ def tile_attention_pa_kernel(tc, x, cos, sin, Wq, Wk, out_0, out_1):
                     out=grouped[:, g, :].bitcast(F32).rearrange(in_order, r=2, u=2),
                     in_=flipped[:].rearrange("kp u r f -> kp %s u" % column_order),
                 )
+            load_raw(j + RAW_BUFS)
+            return grouped
+
+        def quantise(grouped, pool):
             codes = pool.tile([P, PASSES, SLAB], U32, align_bytes=64, name="codes")
             scales = pool.tile([P, PASSES, SLAB], U8, align_bytes=64, name="scales")
             nc.vector.quantize_mx(
@@ -96,25 +101,17 @@ def tile_attention_pa_kernel(tc, x, cos, sin, Wq, Wk, out_0, out_1):
                 scales=scales[:].rearrange("kp g f -> kp (g f)"),
                 in_=grouped[:].rearrange("kp g f -> kp (g f)"),
             )
-            load_raw(j + RAW_BUFS)
             return codes, scales
-
-        w_mx = {}
-
-        def quantise_w_slab(i):
-            if i < len(w_slab_list):
-                w_mx[i] = quantise_slab(2 + i, "f r", w_mx_pool)
 
         for j in range(6):
             load_raw(j)
-        for b in range(2):
-            load_tables(0, b)
-            load_raw(6 + b)
+        load_tables(0, 0)
+        for j in range(6, RAW_BUFS):
+            load_raw(j)
+        load_tables(0, 1)
 
-        x_mx = [quantise_slab(b, "r f", x_mx_pool) for b in range(2)]
-
-        quantise_w_slab(0)
-        quantise_w_slab(1)
+        x_mx = [quantise(transpose_slab(b, "r f"), x_mx_pool) for b in range(2)]
+        w_mx = [quantise(transpose_slab(2 + i, "f r"), w_mx_pool) for i in range(AHEAD)]
         for b in range(2):
             load_tables(1, b)
 
@@ -122,7 +119,6 @@ def tile_attention_pa_kernel(tc, x, cos, sin, Wq, Wk, out_0, out_1):
         for step in range(last_step + 1):
             unit = step // 2
             m, c, s = units[unit]
-            quantise_w_slab(step + 2)
             b = step % 2
             x_codes, x_scales = x_mx[b]
             table_cols = slice(SLAB * s, SLAB * s + SLAB)
@@ -148,6 +144,10 @@ def tile_attention_pa_kernel(tc, x, cos, sin, Wq, Wk, out_0, out_1):
                     in1=tables[c][:, 2 * b + r, :, :, table_cols],
                     op=ALU.mult,
                 )
+                if r == 0 and step + AHEAD < len(w_slab_list):
+                    grouped_ahead = transpose_slab(2 + step + AHEAD, "f r")
+            if step + AHEAD < len(w_slab_list):
+                w_mx.append(quantise(grouped_ahead, w_mx_pool))
             adder = nc.vector if step == last_step else nc.gpsimd
             for h in range(HALVES):
                 result = products[:, :, h, 0, :]

@@ -23,7 +23,6 @@ SLAB = 256
 HALVES = 2
 TABLE_COLS = 512
 TABLE_TILES = D // (HALVES * TABLE_COLS)
-AHEAD = 3
 RAW_BUFS = 8
 
 
@@ -49,7 +48,7 @@ def tile_attention_pa_kernel(tc, x, cos, sin, Wq, Wk, out_0, out_1):
         raw_pool = ctx.enter_context(tc.tile_pool(name="raw", bufs=RAW_BUFS))
         grouped_pool = ctx.enter_context(tc.tile_pool(name="grouped", bufs=3))
         x_mx_pool = ctx.enter_context(tc.tile_pool(name="x_mx", bufs=2))
-        w_mx_pool = ctx.enter_context(tc.tile_pool(name="w_mx", bufs=6))
+        w_mx_pool = ctx.enter_context(tc.tile_pool(name="w_mx", bufs=3))
         products_pool = ctx.enter_context(tc.tile_pool(name="products", bufs=6))
         flipped_pool = ctx.enter_context(tc.psum_pool(name="flipped", bufs=4))
         acc_pool = ctx.enter_context(tc.psum_pool(name="acc", bufs=4))
@@ -76,7 +75,7 @@ def tile_attention_pa_kernel(tc, x, cos, sin, Wq, Wk, out_0, out_1):
             for h in range(HALVES):
                 nc.sync.dma_start(out=tables[c][:, pair, h, 1, :], in_=sin_cols[c][b][:, :, 1 - h, :])
 
-        def transpose_slab(j, column_order):
+        def quantise_slab(j, column_order, codes, scales):
             words = raw_tiles[j][:].bitcast(F32)
             grouped = grouped_pool.tile([P, PASSES, 4 * SLAB], BF16, align_bytes=64)
             in_order = "kp (%s u) -> kp %s u" % (column_order, column_order)
@@ -90,28 +89,37 @@ def tile_attention_pa_kernel(tc, x, cos, sin, Wq, Wk, out_0, out_1):
                     out=grouped[:, g, :].bitcast(F32).rearrange(in_order, r=2, u=2),
                     in_=flipped[:].rearrange("kp u r f -> kp %s u" % column_order),
                 )
+                nc.vector.quantize_mx(
+                    out=codes[:, g, :].bitcast(FP8X4), scales=scales[:, g, :], in_=grouped[:, g, :]
+                )
             load_raw(j + RAW_BUFS)
-            return grouped
 
-        def quantise(grouped, pool):
-            codes = pool.tile([P, PASSES, SLAB], U32, align_bytes=64, name="codes")
-            scales = pool.tile([P, PASSES, SLAB], U8, align_bytes=64, name="scales")
-            nc.vector.quantize_mx(
-                out=codes[:].rearrange("kp g f -> kp (g f)").bitcast(FP8X4),
-                scales=scales[:].rearrange("kp g f -> kp (g f)"),
-                in_=grouped[:].rearrange("kp g f -> kp (g f)"),
-            )
-            return codes, scales
+        w_mx = {}
+
+        def quantise_w_slab(i):
+            if i < len(w_slab_list):
+                if i % HALVES == 0:
+                    w_codes = w_mx_pool.tile([P, PASSES, HALVES, SLAB], U32, align_bytes=64, name="w_codes")
+                    w_scales = w_mx_pool.tile([P, PASSES, HALVES, SLAB], U8, align_bytes=64, name="w_scales")
+                    w_mx[i // HALVES] = (w_codes, w_scales)
+                w_codes, w_scales = w_mx[i // HALVES]
+                quantise_slab(2 + i, "f r", w_codes[:, :, i % HALVES, :], w_scales[:, :, i % HALVES, :])
 
         for j in range(6):
             load_raw(j)
-        load_tables(0, 0)
-        for j in range(6, RAW_BUFS):
-            load_raw(j)
-        load_tables(0, 1)
+        for b in range(2):
+            load_tables(0, b)
+            load_raw(6 + b)
 
-        x_mx = [quantise(transpose_slab(b, "r f"), x_mx_pool) for b in range(2)]
-        w_mx = [quantise(transpose_slab(2 + i, "f r"), w_mx_pool) for i in range(AHEAD)]
+        x_mx = []
+        for b in range(2):
+            x_codes = x_mx_pool.tile([P, PASSES, SLAB], U32, align_bytes=64, name="x_codes")
+            x_scales = x_mx_pool.tile([P, PASSES, SLAB], U8, align_bytes=64, name="x_scales")
+            quantise_slab(b, "r f", x_codes[:], x_scales[:])
+            x_mx.append((x_codes, x_scales))
+
+        quantise_w_slab(0)
+        quantise_w_slab(1)
         for b in range(2):
             load_tables(1, b)
 
@@ -119,35 +127,31 @@ def tile_attention_pa_kernel(tc, x, cos, sin, Wq, Wk, out_0, out_1):
         for step in range(last_step + 1):
             unit = step // 2
             m, c, s = units[unit]
+            quantise_w_slab(step + 2)
             b = step % 2
             x_codes, x_scales = x_mx[b]
+            w_codes, w_scales = w_mx[unit]
             table_cols = slice(SLAB * s, SLAB * s + SLAB)
             products = products_pool.tile([P, 2, HALVES, 2, SLAB], F32)
             for r in range(2):
                 tok = slice(P * r, P * r + P)
                 acc = acc_pool.tile([P, HALVES, SLAB], F32)
-                for h in range(HALVES):
-                    w_codes, w_scales = w_mx[2 * unit + h]
-                    for g in range(PASSES):
-                        nc.tensor.matmul_mx(
-                            out=acc[:, h, :],
-                            lhsT=x_codes[:, g, tok].bitcast(FP8X4),
-                            lhsT_scale=x_scales[:, g, tok],
-                            rhs=w_codes[:, g, :].bitcast(FP8X4),
-                            rhs_scale=w_scales[:, g, :],
-                            start=(g == 0),
-                            stop=(g == PASSES - 1),
-                        )
+                for g in range(PASSES):
+                    nc.tensor.matmul_mx(
+                        out=acc[:].rearrange("p h w -> p (h w)"),
+                        lhsT=x_codes[:, g, tok].bitcast(FP8X4),
+                        lhsT_scale=x_scales[:, g, tok],
+                        rhs=w_codes[:, g].rearrange("kp h w -> kp (h w)").bitcast(FP8X4),
+                        rhs_scale=w_scales[:, g].rearrange("kp h w -> kp (h w)"),
+                        start=(g == 0),
+                        stop=(g == PASSES - 1),
+                    )
                 nc.vector.tensor_tensor(
                     out=products[:, r],
                     in0=acc[:].unsqueeze(2).to_broadcast([P, HALVES, 2, SLAB]),
                     in1=tables[c][:, 2 * b + r, :, :, table_cols],
                     op=ALU.mult,
                 )
-                if r == 0 and step + AHEAD < len(w_slab_list):
-                    grouped_ahead = transpose_slab(2 + step + AHEAD, "f r")
-            if step + AHEAD < len(w_slab_list):
-                w_mx.append(quantise(grouped_ahead, w_mx_pool))
             adder = nc.vector if step == last_step else nc.gpsimd
             for h in range(HALVES):
                 result = products[:, :, h, 0, :]

@@ -38,6 +38,10 @@ def tile_attention_pa_kernel(tc, x, cos, sin, Wq, Wk, out_0, out_1):
     out_cols = [
         o[0].rearrange(out_view, b=2, r=2, h=HALVES, c=TABLE_TILES, w=SLAB) for o in (out_0, out_1)
     ]
+    wide_view = "(p b r) (h c w) -> c b p r h w"
+    out_wide = [
+        o[0].rearrange(wide_view, b=2, r=2, h=HALVES, c=TABLE_TILES) for o in (out_0, out_1)
+    ]
 
     units = [(m, c, s) for c in range(TABLE_TILES) for m in range(2) for s in range(2)]
     w_slab_list = [(m, 4 * h + 2 * c + s) for (m, c, s) in units for h in range(HALVES)]
@@ -49,7 +53,8 @@ def tile_attention_pa_kernel(tc, x, cos, sin, Wq, Wk, out_0, out_1):
         grouped_pool = ctx.enter_context(tc.tile_pool(name="grouped", bufs=3))
         x_mx_pool = ctx.enter_context(tc.tile_pool(name="x_mx", bufs=2))
         w_mx_pool = ctx.enter_context(tc.tile_pool(name="w_mx", bufs=3))
-        products_pool = ctx.enter_context(tc.tile_pool(name="products", bufs=6))
+        products_pool = ctx.enter_context(tc.tile_pool(name="products", bufs=4))
+        results_pool = ctx.enter_context(tc.tile_pool(name="results", bufs=4))
         flipped_pool = ctx.enter_context(tc.psum_pool(name="flipped", bufs=4))
         acc_pool = ctx.enter_context(tc.psum_pool(name="acc", bufs=4))
         ctx.enter_context(tc.manual_schedule())
@@ -124,6 +129,7 @@ def tile_attention_pa_kernel(tc, x, cos, sin, Wq, Wk, out_0, out_1):
             load_tables(1, b)
 
         last_step = 2 * len(units) - 1
+        results = {}
         for step in range(last_step + 1):
             unit = step // 2
             m, c, s = units[unit]
@@ -153,12 +159,17 @@ def tile_attention_pa_kernel(tc, x, cos, sin, Wq, Wk, out_0, out_1):
                     op=ALU.mult,
                 )
             adder = nc.vector if step == last_step else nc.gpsimd
+            if s == 0:
+                results[b] = results_pool.tile([P, 2, HALVES, TABLE_COLS], F32, name="result")
             for h in range(HALVES):
-                result = products[:, :, h, 0, :]
                 adder.tensor_tensor(
-                    out=result,
-                    in0=result,
+                    out=results[b][:, :, h, table_cols],
+                    in0=products[:, :, h, 0, :],
                     in1=products[:, :, 1 - h, 1, :],
                     op=(ALU.subtract if h == 0 else ALU.add),
                 )
-                nc.sync.dma_start(out=out_cols[m][c][s][b][h], in_=result)
+                if unit >= len(units) - 2:
+                    nc.sync.dma_start(out=out_cols[m][c][s][b][h], in_=results[b][:, :, h, table_cols])
+            if unit < len(units) - 2 and s == 1:
+                for r in range(2):
+                    nc.sync.dma_start(out=out_wide[m][c][b][:, r], in_=results[b][:, r])

from contextlib import ExitStack

import concourse.mybir as mybir
from concourse.masks import make_identity

BF16 = mybir.dt.bfloat16
F32 = mybir.dt.float32
U32 = mybir.dt.uint32
U8 = mybir.dt.uint8
FP8X4 = mybir.dt.float8_e4m3fn_x4
ALU = mybir.AluOpType

P = 128
TOKENS = 512
D = 2048
FLOPS = 2 * 2 * TOKENS * D * D

TOKEN_TILES = TOKENS // P
K_PASS = 4 * P
PASSES = D // K_PASS
WORDS = K_PASS // 2
SLAB = 256
HALVES = 2
TABLE_COLS = 512
TABLE_TILES = D // (HALVES * TABLE_COLS)
RAW_BUFS = 8


def tile_attention_pa_kernel(tc, x, cos, sin, Wq, Wk, out_0, out_1):
    nc = tc.nc

    x_slabs = x[0].rearrange("(p b r) k -> b p r k", b=2, r=2)
    w_slabs = [w.rearrange("(n p r) k -> n p r k", p=P, r=2) for w in (Wq, Wk)]
    table_view = "(p b r) (h c w) -> c b p r h w"
    cos_cols = cos.rearrange(table_view, b=2, r=2, h=HALVES, c=TABLE_TILES)
    sin_cols = sin.rearrange(table_view, b=2, r=2, h=HALVES, c=TABLE_TILES)
    out_view = "(p b r) (h c s w) -> c s b h p r w"
    out_cols = [
        o[0].rearrange(out_view, b=2, r=2, h=HALVES, c=TABLE_TILES, w=SLAB) for o in (out_0, out_1)
    ]
    wide_view = "(p b r) (h c w) -> c b p r h w"
    out_wide = [
        o[0].rearrange(wide_view, b=2, r=2, h=HALVES, c=TABLE_TILES) for o in (out_0, out_1)
    ]

    units = [(m, c, s) for c in range(TABLE_TILES) for m in range(2) for s in range(2)]
    w_slab_list = [(m, 4 * h + 2 * c + s) for (m, c, s) in units for h in range(HALVES)]
    raw_sources = [x_slabs[0], x_slabs[1]] + [w_slabs[m][n] for (m, n) in w_slab_list]

    with ExitStack() as ctx:
        const = ctx.enter_context(tc.tile_pool(name="const", bufs=1))
        raw_pool = ctx.enter_context(tc.tile_pool(name="raw", bufs=RAW_BUFS))
        grouped_pool = ctx.enter_context(tc.tile_pool(name="grouped", bufs=3))
        x_mx_pool = ctx.enter_context(tc.tile_pool(name="x_mx", bufs=2))
        w_mx_pool = ctx.enter_context(tc.tile_pool(name="w_mx", bufs=3))
        products_pool = ctx.enter_context(tc.tile_pool(name="products", bufs=4))
        results_pool = ctx.enter_context(tc.tile_pool(name="results", bufs=4))
        flipped_pool = ctx.enter_context(tc.psum_pool(name="flipped", bufs=4))
        acc_pool = ctx.enter_context(tc.psum_pool(name="acc", bufs=4))
        ctx.enter_context(tc.manual_schedule())

        ident = const.tile([P, P], F32)
        make_identity(nc, ident[:])
        tables = [
            const.tile([P, TOKEN_TILES, HALVES, 2, TABLE_COLS], BF16, name="tables%d" % c)
            for c in range(TABLE_TILES)
        ]

        raw_tiles = {}

        def load_raw(j):
            if j < len(raw_sources):
                raw = raw_pool.tile([P, 2, D], BF16, name="raw")
                nc.sync.dma_start(out=raw[:], in_=raw_sources[j])
                raw_tiles[j] = raw

        def load_tables(c, b):
            pair = slice(2 * b, 2 * b + 2)
            nc.sync.dma_start(out=tables[c][:, pair, :, 0, :], in_=cos_cols[c][b])
            for h in range(HALVES):
                nc.sync.dma_start(out=tables[c][:, pair, h, 1, :], in_=sin_cols[c][b][:, :, 1 - h, :])

        def quantise_slab(j, column_order, codes, scales):
            words = raw_tiles[j][:].bitcast(F32)
            grouped = grouped_pool.tile([P, PASSES, 4 * SLAB], BF16, align_bytes=64)
            in_order = "kp (%s u) -> kp %s u" % (column_order, column_order)
            for g in range(PASSES):
                flipped = flipped_pool.tile([P, 2, 2, P], F32)
                for u in range(2):
                    for r in range(2):
                        lo = WORDS * g + P * u
                        nc.tensor.transpose(flipped[:, u, r, :], words[:, r, lo : lo + P], ident[:])
                nc.scalar.copy(
                    out=grouped[:, g, :].bitcast(F32).rearrange(in_order, r=2, u=2),
                    in_=flipped[:].rearrange("kp u r f -> kp %s u" % column_order),
                )
                nc.vector.quantize_mx(
                    out=codes[:, g, :].bitcast(FP8X4), scales=scales[:, g, :], in_=grouped[:, g, :]
                )
            load_raw(j + RAW_BUFS)

        w_mx = {}

        def quantise_w_slab(i):
            if i < len(w_slab_list):
                if i % HALVES == 0:
                    w_codes = w_mx_pool.tile([P, PASSES, HALVES, SLAB], U32, align_bytes=64, name="w_codes")
                    w_scales = w_mx_pool.tile([P, PASSES, HALVES, SLAB], U8, align_bytes=64, name="w_scales")
                    w_mx[i // HALVES] = (w_codes, w_scales)
                w_codes, w_scales = w_mx[i // HALVES]
                quantise_slab(2 + i, "f r", w_codes[:, :, i % HALVES, :], w_scales[:, :, i % HALVES, :])

        for j in range(6):
            load_raw(j)
        for b in range(2):
            load_tables(0, b)
            load_raw(6 + b)

        x_mx = []
        for b in range(2):
            x_codes = x_mx_pool.tile([P, PASSES, SLAB], U32, align_bytes=64, name="x_codes")
            x_scales = x_mx_pool.tile([P, PASSES, SLAB], U8, align_bytes=64, name="x_scales")
            quantise_slab(b, "r f", x_codes[:], x_scales[:])
            x_mx.append((x_codes, x_scales))

        quantise_w_slab(0)
        quantise_w_slab(1)
        for b in range(2):
            load_tables(1, b)

        last_step = 2 * len(units) - 1
        results = {}
        for step in range(last_step + 1):
            unit = step // 2
            m, c, s = units[unit]
            quantise_w_slab(step + 2)
            b = step % 2
            x_codes, x_scales = x_mx[b]
            w_codes, w_scales = w_mx[unit]
            table_cols = slice(SLAB * s, SLAB * s + SLAB)
            products = products_pool.tile([P, 2, HALVES, 2, SLAB], F32)
            for r in range(2):
                tok = slice(P * r, P * r + P)
                acc = acc_pool.tile([P, HALVES, SLAB], F32)
                for g in range(PASSES):
                    nc.tensor.matmul_mx(
                        out=acc[:].rearrange("p h w -> p (h w)"),
                        lhsT=x_codes[:, g, tok].bitcast(FP8X4),
                        lhsT_scale=x_scales[:, g, tok],
                        rhs=w_codes[:, g].rearrange("kp h w -> kp (h w)").bitcast(FP8X4),
                        rhs_scale=w_scales[:, g].rearrange("kp h w -> kp (h w)"),
                        start=(g == 0),
                        stop=(g == PASSES - 1),
                    )
                nc.vector.tensor_tensor(
                    out=products[:, r],
                    in0=acc[:].unsqueeze(2).to_broadcast([P, HALVES, 2, SLAB]),
                    in1=tables[c][:, 2 * b + r, :, :, table_cols],
                    op=ALU.mult,
                )
            adder = nc.vector if step == last_step else nc.gpsimd
            if s == 0:
                results[b] = results_pool.tile([P, 2, HALVES, TABLE_COLS], F32, name="result")
            for h in range(HALVES):
                adder.tensor_tensor(
                    out=results[b][:, :, h, table_cols],
                    in0=products[:, :, h, 0, :],
                    in1=products[:, :, 1 - h, 1, :],
                    op=(ALU.subtract if h == 0 else ALU.add),
                )
                if unit >= len(units) - 2:
                    nc.sync.dma_start(out=out_cols[m][c][s][b][h], in_=results[b][:, :, h, table_cols])
            if unit < len(units) - 2 and s == 1:
                for r in range(2):
                    nc.sync.dma_start(out=out_wide[m][c][b][:, r], in_=results[b][:, r])
